import numpy as np
import ml_dtypes


def mxq(x, axis, fmt="e4m3"):
    dtype, down = {"e4m3": (ml_dtypes.float8_e4m3fn, 7), "e5m2": (ml_dtypes.float8_e5m2, 14)}[fmt]
    v = np.moveaxis(np.asarray(x, np.float32).astype(ml_dtypes.bfloat16).astype(np.float64), axis, -1)
    blocks = v.reshape(v.shape[:-1] + (-1, 32))
    amax = np.abs(blocks).max(-1, keepdims=True)
    byte = np.maximum(np.where(amax > 0, np.frexp(amax)[1] - 1 + 127, 0) - down, 1)
    scale = np.exp2(byte - 127.0)
    codes = (blocks / scale).astype(np.float32).astype(dtype).astype(np.float64)
    return np.moveaxis((codes * scale).reshape(v.shape), -1, axis)


WIDE = False


def mx_kscale(k):
    if not WIDE:
        return np.ones(k)
    levels = np.array([10, -10, 5, -5, 0])
    if k % 512:
        return np.exp2(np.random.permutation(np.resize(levels, k // 32))).repeat(32)
    a = np.empty((k // 512, 16))
    for p in range(k // 512):
        a[p, :8] = np.random.permutation(np.resize(levels, 8))
        for g in range(8):
            far = levels[np.abs(levels - a[p, g]) >= 10]
            a[p, g + 8] = far[np.random.randint(len(far))]
    return np.exp2(a.ravel()).repeat(32)


BF16 = ml_dtypes.bfloat16


def bf(x):
    return np.asarray(x, np.float32).astype(BF16)


def f64(x):
    return np.asarray(x).astype(np.float64)


B, T, H, DK, DH, E, V = 4, 1024, 8, 64, 64, 1024, 1536
HK = H * DK


def rotate_every_two(u):
    u1 = u[..., ::2]
    u2 = u[..., 1::2]
    return np.stack((-u2, u1), axis=-1).reshape(u.shape)


def theta_shift(u, sin, cos):
    return u * cos + rotate_every_two(u) * sin


def setup_inputs():
    s = mx_kscale(E)
    return {"x": bf(np.random.standard_normal((B, T, E)) * s),
            "sin": bf(np.random.standard_normal((T, DK)) * 0.7),
            "cos": bf(np.random.standard_normal((T, DK)) * 0.7),
            "Wq": bf(np.random.standard_normal((E, HK)) / np.sqrt(E) / s[:, None]),
            "Wk": bf(np.random.standard_normal((E, HK)) / np.sqrt(E) / s[:, None])}


def reference(x, sin, cos, Wq, Wk):
    xq = mxq(f64(x), 2, "e4m3")
    q = (xq @ mxq(f64(Wq), 0, "e4m3")).reshape(B, T, H, DK).transpose(0, 2, 1, 3)
    k = (xq @ mxq(f64(Wk), 0, "e4m3")).reshape(B, T, H, DK).transpose(0, 2, 1, 3)
    qr = theta_shift(q, f64(sin), f64(cos))
    kr = theta_shift(k, f64(sin), f64(cos))
    return qr, kr

@@ -1,0 +1,289 @@
+from contextlib import ExitStack
+
+import concourse.mybir as mybir
+from concourse.masks import make_identity
+
+F32 = mybir.dt.float32
+BF16 = mybir.dt.bfloat16
+U32 = mybir.dt.uint32
+U8 = mybir.dt.uint8
+FP8X4 = mybir.dt.float8_e4m3fn_x4
+MULT = mybir.AluOpType.mult
+ADD = mybir.AluOpType.add
+
+P = 128
+SEQS, TOKENS, E = 4, 1024, 1024
+HEADS, CHANNELS = 8, 64
+COLS = HEADS * CHANNELS
+HALF = CHANNELS // 2
+PLANE = HEADS * HALF
+TOK_PP = TOKENS // P
+WORDS = E // 2
+PASSES = 2
+PACK = 4
+PAIRS_PER_SEQ = TOK_PP // 2
+PAIRS = SEQS * PAIRS_PER_SEQ
+UNITS_PER_SEQ = 2 * PAIRS_PER_SEQ
+UNITS = SEQS * UNITS_PER_SEQ
+BLOCKS = UNITS // 2
+BLOCK_TOK = 4
+Q, K = 0, 1
+FIRST_K_UNIT = PAIRS_PER_SEQ
+AHEAD = 2
+
+FLOPS = 2 * SEQS * TOKENS * E * 2 * COLS
+
+
+def tile_multiscaleretention_pa_t_kernel(tc, x, sin, cos, Wq, Wk, out_0, out_1):
+    nc = tc.nc
+    with ExitStack() as ctx:
+        const = ctx.enter_context(tc.tile_pool(name="const", bufs=1))
+        xpool = ctx.enter_context(tc.tile_pool(name="xpool", bufs=SEQS))
+        stage = ctx.enter_context(tc.tile_pool(name="stage", bufs=3))
+        codes = ctx.enter_context(tc.tile_pool(name="codes", bufs=2))
+        prod = ctx.enter_context(tc.tile_pool(name="prod", bufs=3))
+        opool = ctx.enter_context(tc.tile_pool(name="opool", bufs=4))
+        tpsum = ctx.enter_context(tc.psum_pool(name="tpsum", bufs=2))
+        acc = ctx.enter_context(tc.psum_pool(name="acc", bufs=3))
+
+        ident = const.tile([P, P], F32, name="ident")
+        make_identity(nc, ident[:])
+
+        ctx.enter_context(tc.manual_schedule())
+
+        warm_in = const.tile([P, 8], F32, name="warm_in")
+        warm_out = const.tile([P, 8], F32, name="warm_out")
+        nc.vector.memset(warm_in[:], 0.0)
+        nc.scalar.copy(out=warm_out[:], in_=warm_in[:])
+
+        x_sb = [xpool.tile([P, TOK_PP * E], BF16, name="x_sb", tag="x_sb") for b in range(SEQS)]
+        x_dram = [x[b].rearrange("(p j) k -> p (j k)", j=TOK_PP) for b in range(SEQS)]
+        w_sb = [const.tile([P, PASSES * PACK, COLS], BF16, name="w_sb%d" % qk) for qk in (Q, K)]
+        w_dram = [w.rearrange("(g p t) c -> p g t c", g=PASSES, p=P, t=PACK) for w in (Wq, Wk)]
+        cos_sb = const.tile([P, TOK_PP, CHANNELS], BF16, name="cos_sb")
+        sin_sb = const.tile([P, TOK_PP, CHANNELS], BF16, name="sin_sb")
+
+        def load_w(qk, g):
+            nc.sync.dma_start(
+                out=w_sb[qk][:, PACK * g : PACK * (g + 1), :],
+                in_=w_dram[qk][:, g],
+            )
+
+        first = 2 * E
+        nc.sync.dma_start(out=x_sb[0][:, 0:first], in_=x_dram[0][:, 0:first])
+        load_w(Q, 0)
+        load_w(Q, 1)
+        nc.sync.dma_start(out=cos_sb[:], in_=cos.rearrange("(p j) c -> p j c", j=TOK_PP))
+        nc.sync.dma_start(out=sin_sb[:], in_=sin.rearrange("(p j) c -> p j c", j=TOK_PP))
+        load_w(K, 0)
+        nc.sync.dma_start(out=x_sb[0][:, first:], in_=x_dram[0][:, first:])
+        load_w(K, 1)
+        for b in range(1, SEQS):
+            nc.sync.dma_start(out=x_sb[b][:], in_=x_dram[b])
+
+        COS_EVEN, COS_ODD, NEG_SIN_EVEN, SIN_ODD = 0, 1, 2, 3
+        tab = const.tile([P, 4, TOK_PP, HALF], F32, name="tab")
+        cos_planes = cos_sb[:].rearrange("p t (i j) -> p j t i", j=2)
+        sin_planes = sin_sb[:].rearrange("p t (i j) -> p j t i", j=2)
+        nc.gpsimd.tensor_scalar(
+            out=tab[:, COS_EVEN : COS_ODD + 1], in0=cos_planes, scalar1=1.0, scalar2=0.0, op0=MULT, op1=ADD
+        )
+        nc.gpsimd.tensor_scalar(
+            out=tab[:, NEG_SIN_EVEN], in0=sin_planes[:, 0], scalar1=-1.0, scalar2=0.0, op0=MULT, op1=ADD
+        )
+        nc.gpsimd.tensor_scalar(
+            out=tab[:, SIN_ODD], in0=sin_planes[:, 1], scalar1=1.0, scalar2=0.0, op0=MULT, op1=ADD
+        )
+
+        w_codes = const.tile([P, PASSES, 2, COLS], U32, name="w_codes", align_bytes=64)
+        w_scales = const.tile([P, PASSES, 2, COLS], U8, name="w_scales", align_bytes=64)
+        w_grp = {}
+
+        def regroup_w(qk, g, j, copy):
+            if (qk, g) not in w_grp:
+                w_grp[(qk, g)] = stage.tile(
+                    [P, 2, PLANE, PACK], BF16, name="w_grp", tag="w_grp", bufs=2 * PASSES, align_bytes=64
+                )
+            rows = w_sb[qk][:, PACK * g : PACK * (g + 1), :].rearrange("p t (r j) -> p j r t", j=2)
+            copy(out=w_grp[(qk, g)][:, j], in_=rows[:, j])
+
+        def quantise_w(qk, g):
+            nc.vector.quantize_mx(
+                out=w_codes[:, g, qk, :].bitcast(FP8X4),
+                scales=w_scales[:, g, qk, :],
+                in_=w_grp[(qk, g)][:].rearrange("p j r t -> p (j r t)"),
+            )
+
+        x_grp = {}
+        x_codes = {}
+        x_scales = {}
+
+        def transpose_pair(pair):
+            b, r = divmod(pair, PAIRS_PER_SEQ)
+            words = x_sb[b][:].bitcast(F32)
+            x_grp[pair] = stage.tile([P, 2 * WORDS], F32, name="x_grp", tag="x_grp", align_bytes=64)
+            banks = []
+            for s in range(2):
+                bank = tpsum.tile([P, 2 * PASSES, P], F32, name="bank_t", tag="bank_t")
+                for a in range(2 * PASSES):
+                    g, u = divmod(a, 2)
+                    lo = (2 * r + s) * WORDS + g * 2 * P
+                    nc.tensor.transpose(bank[:, a, :], words[:, lo + u : lo + 2 * P : 2], ident[:])
+                banks.append(bank)
+            return banks
+
+        def copy_out(pair, s, bank, copy):
+            copy(
+                out=x_grp[pair][:, s * WORDS : (s + 1) * WORDS].rearrange("p (g k u) -> p g k u", g=PASSES, u=2),
+                in_=bank[:].rearrange("p (g u) k -> p g k u", u=2),
+            )
+
+        def prepare_pair(pair):
+            banks = transpose_pair(pair)
+            for s in range(2):
+                copy_out(pair, s, banks[s], nc.scalar.copy)
+
+        def quantise_x(pair):
+            b, r = divmod(pair, PAIRS_PER_SEQ)
+            if r == 0:
+                x_codes[b] = codes.tile([P, TOK_PP * PASSES * P], U32, name="x_codes", tag="x_codes", align_bytes=64)
+                x_scales[b] = codes.tile([P, TOK_PP * PASSES * P], U8, name="x_scales", tag="x_scales", align_bytes=64)
+            lo = r * 2 * PASSES * P
+            nc.vector.quantize_mx(
+                out=x_codes[b][:, lo : lo + 2 * PASSES * P].bitcast(FP8X4),
+                scales=x_scales[b][:, lo : lo + 2 * PASSES * P],
+                in_=x_grp[pair][:].bitcast(BF16),
+            )
+
+        banks_of = {}
+        products_of = {}
+
+        def unit_key(u):
+            b, rest = divmod(u, UNITS_PER_SEQ)
+            qk, r = divmod(rest, PAIRS_PER_SEQ)
+            return b, qk, r
+
+        def matmuls(u):
+            b, qk, r = unit_key(u)
+            bank_e = acc.tile([P, 2 * PLANE], F32, name="bank_e", tag="bank_e")
+            bank_o = acc.tile([P, 2 * PLANE], F32, name="bank_o", tag="bank_o")
+            banks_of[u] = (bank_e, bank_o)
+            for s in range(2):
+                for j in range(2):
+                    for g in range(PASSES):
+                        lo = ((2 * r + s) * PASSES + g) * P
+                        nc.tensor.matmul_mx(
+                            out=banks_of[u][j][:, PLANE * s : PLANE * (s + 1)],
+                            lhsT=x_codes[b][:, lo : lo + P].bitcast(FP8X4),
+                            lhsT_scale=x_scales[b][:, lo : lo + P],
+                            rhs=w_codes[:, g, qk, PLANE * j : PLANE * (j + 1)].bitcast(FP8X4),
+                            rhs_scale=w_scales[:, g, qk, PLANE * j : PLANE * (j + 1)],
+                            start=(g == 0),
+                            stop=(g == PASSES - 1),
+                        )
+
+        def products(u):
+            r = unit_key(u)[2]
+            if u % 2 == 0:
+                first_p = prod.tile([P, 2, HEADS, BLOCK_TOK, HALF], F32, name="first_p", tag="first_p")
+                second_p = prod.tile([P, 2, HEADS, BLOCK_TOK, HALF], F32, name="second_p", tag="second_p")
+                products_of[u // 2] = (first_p, second_p)
+            first_p, second_p = products_of[u // 2]
+            lo = 2 * (u % 2)
+
+            def multiply(dst, j, bank, table):
+                nc.vector.tensor_tensor(
+                    out=dst[:, j, :, lo : lo + 2, :].rearrange("p h t i -> p t h i"),
+                    in0=bank[:].rearrange("p (t h i) -> p t h i", t=2, h=HEADS),
+                    in1=tab[:, table, 2 * r : 2 * r + 2, :].unsqueeze(2).to_broadcast([P, 2, HEADS, HALF]),
+                    op=MULT,
+                )
+
+            bank_e, bank_o = banks_of[u]
+            multiply(first_p, 0, bank_e, COS_EVEN)
+            multiply(second_p, 1, bank_e, SIN_ODD)
+            multiply(first_p, 1, bank_o, COS_ODD)
+            multiply(second_p, 0, bank_o, NEG_SIN_EVEN)
+
+        def out_rows(k):
+            b, qk, r = unit_key(2 * k)
+            rows = (out_0, out_1)[qk][b].rearrange("h (p t) c -> p h t c", t=TOK_PP)
+            return rows[:, :, 2 * r : 2 * r + BLOCK_TOK, :]
+
+        def interleaved(tile_ap):
+            return tile_ap.rearrange("p h t (i j) -> p h (t i) j", j=2)
+
+        def planes(tile_ap):
+            return tile_ap.rearrange("p j h t i -> p h (t i) j")
+
+        def sum_on_gpsimd(k):
+            first_p, second_p = products_of[k]
+            o_sb = opool.tile([P, HEADS, BLOCK_TOK, CHANNELS], F32, name="o_sb", tag="o_sb")
+            nc.gpsimd.tensor_tensor(
+                out=first_p[:].rearrange("p j h t i -> p (j h t i)"),
+                in0=first_p[:].rearrange("p j h t i -> p (j h t i)"),
+                in1=second_p[:].rearrange("p j h t i -> p (j h t i)"),
+                op=ADD,
+            )
+            nc.scalar.copy(out=interleaved(o_sb[:]), in_=planes(first_p[:]))
+            return o_sb
+
+        def sum_on_vector_and_store(k):
+            first_p, second_p = products_of[k]
+            o_sb = opool.tile([P, HEADS, BLOCK_TOK, CHANNELS], F32, name="o_sb", tag="o_sb")
+            for lo in (0, 2):
+                nc.vector.tensor_tensor(
+                    out=interleaved(o_sb[:, :, lo : lo + 2, :]),
+                    in0=planes(first_p[:, :, :, lo : lo + 2, :]),
+                    in1=planes(second_p[:, :, :, lo : lo + 2, :]),
+                    op=ADD,
+                )
+                nc.sync.dma_start(out=out_rows(k)[:, :, lo : lo + 2, :], in_=o_sb[:, :, lo : lo + 2, :])
+
+
+        prepare_pair(0)
+        regroup_w(Q, 0, 0, nc.vector.tensor_copy)
+        regroup_w(Q, 0, 1, nc.vector.tensor_copy)
+        regroup_w(Q, 1, 0, nc.vector.tensor_copy)
+        regroup_w(Q, 1, 1, nc.scalar.copy)
+        quantise_x(0)
+        quantise_w(Q, 0)
+        quantise_w(Q, 1)
+        matmuls(0)
+        regroup_w(K, 0, 0, nc.vector.tensor_copy)
+        regroup_w(K, 0, 1, nc.vector.tensor_copy)
+
+        issued = 1
+        held = None
+        for u in range(UNITS):
+            products(u)
+            k = u // 2
+            if u == 0:
+                for pair in range(1, PAIRS_PER_SEQ):
+                    banks = transpose_pair(pair)
+                    copy_out(pair, 0, banks[0], nc.scalar.copy)
+                    copy_out(pair, 1, banks[1], nc.vector.tensor_copy)
+                    quantise_x(pair)
+                regroup_w(K, 1, 0, nc.scalar.copy)
+                regroup_w(K, 1, 1, nc.scalar.copy)
+            if u == FIRST_K_UNIT - 1:
+                quantise_w(K, 0)
+                quantise_w(K, 1)
+            if u % 2 == 1 and PAIRS_PER_SEQ <= k + 3 < PAIRS:
+                quantise_x(k + 3)
+            while issued < UNITS and issued <= u + AHEAD and (issued < FIRST_K_UNIT or u >= FIRST_K_UNIT - 1):
+                matmuls(issued)
+                issued += 1
+            if u == 1:
+                prepare_pair(PAIRS_PER_SEQ)
+            if u % 2 == 1 and k + 5 < PAIRS:
+                prepare_pair(k + 5)
+            if u % 2 == 1:
+                if k < BLOCKS - 2:
+                    o_sb = sum_on_gpsimd(k)
+                    nc.sync.dma_start(out=out_rows(k), in_=o_sb[:])
+                elif k == BLOCKS - 2:
+                    held = sum_on_gpsimd(k)
+                else:
+                    sum_on_vector_and_store(k)
+                    nc.sync.dma_start(out=out_rows(k - 1), in_=held[:])

@@ -10,26 +10,24 @@ U8 = mybir.dt.uint8
 FP8X4 = mybir.dt.float8_e4m3fn_x4
 MULT = mybir.AluOpType.mult
 ADD = mybir.AluOpType.add
+COPY = mybir.ActivationFunctionType.Copy
 
 P = 128
 SEQS, TOKENS, E = 4, 1024, 1024
 HEADS, CHANNELS = 8, 64
 COLS = HEADS * CHANNELS
-HALF = CHANNELS // 2
-PLANE = HEADS * HALF
+ROWS = 2 * HEADS
 TOK_PP = TOKENS // P
 WORDS = E // 2
 PASSES = 2
 PACK = 4
 PAIRS_PER_SEQ = TOK_PP // 2
 PAIRS = SEQS * PAIRS_PER_SEQ
-UNITS_PER_SEQ = 2 * PAIRS_PER_SEQ
-UNITS = SEQS * UNITS_PER_SEQ
-BLOCKS = UNITS // 2
-BLOCK_TOK = 4
-Q, K = 0, 1
-FIRST_K_UNIT = PAIRS_PER_SEQ
-AHEAD = 2
+TILES = 2 * PAIRS
+STORE_TOK = 4
+CA, CB, CS = 32, 24, 8
+CV = CA + CB
+LO_A, LO_B, LO_S = 0, ROWS * CA, ROWS * CV
 
 FLOPS = 2 * SEQS * TOKENS * E * 2 * COLS
 
@@ -39,251 +37,265 @@ def tile_multiscaleretention_pa_t_kernel(tc, x, sin, cos, Wq, Wk, out_0, out_1):
     with ExitStack() as ctx:
         const = ctx.enter_context(tc.tile_pool(name="const", bufs=1))
         xpool = ctx.enter_context(tc.tile_pool(name="xpool", bufs=SEQS))
-        stage = ctx.enter_context(tc.tile_pool(name="stage", bufs=3))
-        codes = ctx.enter_context(tc.tile_pool(name="codes", bufs=2))
+        stage = ctx.enter_context(tc.tile_pool(name="stage", bufs=4))
+        codes = ctx.enter_context(tc.tile_pool(name="codes", bufs=4))
         prod = ctx.enter_context(tc.tile_pool(name="prod", bufs=3))
         opool = ctx.enter_context(tc.tile_pool(name="opool", bufs=4))
         tpsum = ctx.enter_context(tc.psum_pool(name="tpsum", bufs=2))
-        acc = ctx.enter_context(tc.psum_pool(name="acc", bufs=3))
+        acc = ctx.enter_context(tc.psum_pool(name="acc", bufs=2))
 
         ident = const.tile([P, P], F32, name="ident")
         make_identity(nc, ident[:])
-
         ctx.enter_context(tc.manual_schedule())
 
         warm_in = const.tile([P, 8], F32, name="warm_in")
         warm_out = const.tile([P, 8], F32, name="warm_out")
         nc.vector.memset(warm_in[:], 0.0)
-        nc.scalar.copy(out=warm_out[:], in_=warm_in[:])
+        nc.scalar.activation(out=warm_out[:], in_=warm_in[:], func=COPY, scale=warm_in[:, 0:1])
 
-        x_sb = [xpool.tile([P, TOK_PP * E], BF16, name="x_sb", tag="x_sb") for b in range(SEQS)]
-        x_dram = [x[b].rearrange("(p j) k -> p (j k)", j=TOK_PP) for b in range(SEQS)]
-        w_sb = [const.tile([P, PASSES * PACK, COLS], BF16, name="w_sb%d" % qk) for qk in (Q, K)]
+        x_sb = [xpool.tile([P, TOK_PP, E], BF16, name="x_sb", tag="x_sb") for b in range(SEQS)]
+        x_dram = [x[b].rearrange("(p j) k -> p j k", j=TOK_PP) for b in range(SEQS)]
+        w_sb = [const.tile([P, PASSES, PACK, COLS], BF16, name="w_sb%d" % qk) for qk in range(2)]
         w_dram = [w.rearrange("(g p t) c -> p g t c", g=PASSES, p=P, t=PACK) for w in (Wq, Wk)]
         cos_sb = const.tile([P, TOK_PP, CHANNELS], BF16, name="cos_sb")
         sin_sb = const.tile([P, TOK_PP, CHANNELS], BF16, name="sin_sb")
 
-        def load_w(qk, g):
-            nc.sync.dma_start(
-                out=w_sb[qk][:, PACK * g : PACK * (g + 1), :],
-                in_=w_dram[qk][:, g],
-            )
+        def load_x(b, lo, hi):
+            nc.sync.dma_start(out=x_sb[b][:, lo:hi, :], in_=x_dram[b][:, lo:hi, :])
 
-        first = 2 * E
-        nc.sync.dma_start(out=x_sb[0][:, 0:first], in_=x_dram[0][:, 0:first])
-        load_w(Q, 0)
-        load_w(Q, 1)
+        load_x(0, 0, 2)
+        for g in range(PASSES):
+            for qk in range(2):
+                nc.sync.dma_start(out=w_sb[qk][:, g], in_=w_dram[qk][:, g])
         nc.sync.dma_start(out=cos_sb[:], in_=cos.rearrange("(p j) c -> p j c", j=TOK_PP))
         nc.sync.dma_start(out=sin_sb[:], in_=sin.rearrange("(p j) c -> p j c", j=TOK_PP))
-        load_w(K, 0)
-        nc.sync.dma_start(out=x_sb[0][:, first:], in_=x_dram[0][:, first:])
-        load_w(K, 1)
+        load_x(0, 2, 4)
+        load_x(0, 4, 8)
         for b in range(1, SEQS):
-            nc.sync.dma_start(out=x_sb[b][:], in_=x_dram[b])
+            load_x(b, 0, 4)
+            load_x(b, 4, 8)
 
-        COS_EVEN, COS_ODD, NEG_SIN_EVEN, SIN_ODD = 0, 1, 2, 3
-        tab = const.tile([P, 4, TOK_PP, HALF], F32, name="tab")
-        cos_planes = cos_sb[:].rearrange("p t (i j) -> p j t i", j=2)
-        sin_planes = sin_sb[:].rearrange("p t (i j) -> p j t i", j=2)
-        nc.gpsimd.tensor_scalar(
-            out=tab[:, COS_EVEN : COS_ODD + 1], in0=cos_planes, scalar1=1.0, scalar2=0.0, op0=MULT, op1=ADD
-        )
-        nc.gpsimd.tensor_scalar(
-            out=tab[:, NEG_SIN_EVEN], in0=sin_planes[:, 0], scalar1=-1.0, scalar2=0.0, op0=MULT, op1=ADD
-        )
-        nc.gpsimd.tensor_scalar(
-            out=tab[:, SIN_ODD], in0=sin_planes[:, 1], scalar1=1.0, scalar2=0.0, op0=MULT, op1=ADD
-        )
+        cos_f = const.tile([P, TOK_PP, CHANNELS], F32, name="cos_f")
+        sin_f = const.tile([P, TOK_PP, CHANNELS], F32, name="sin_f")
+        nc.gpsimd.tensor_scalar(out=cos_f[:], in0=cos_sb[:], scalar1=1.0, scalar2=0.0, op0=MULT, op1=ADD)
+        for par, sign in ((0, -1.0), (1, 1.0)):
+            nc.gpsimd.tensor_scalar(
+                out=sin_f[:].rearrange("p t (i e) -> p e t i", e=2)[:, par],
+                in0=sin_sb[:].rearrange("p t (i e) -> p e t i", e=2)[:, par],
+                scalar1=sign,
+                scalar2=0.0,
+                op0=MULT,
+                op1=ADD,
+            )
 
-        w_codes = const.tile([P, PASSES, 2, COLS], U32, name="w_codes", align_bytes=64)
-        w_scales = const.tile([P, PASSES, 2, COLS], U8, name="w_scales", align_bytes=64)
-        w_grp = {}
+        w_grp = [const.tile([P, ROWS * CHANNELS, PACK], BF16, name="w_grp%d" % g, align_bytes=64) for g in range(PASSES)]
+        w_codes = const.tile([P, PASSES, ROWS * CHANNELS], U32, name="w_codes", align_bytes=64)
+        w_scales = const.tile([P, PASSES, ROWS * CHANNELS], U8, name="w_scales", align_bytes=64)
 
-        def regroup_w(qk, g, j, copy):
-            if (qk, g) not in w_grp:
-                w_grp[(qk, g)] = stage.tile(
-                    [P, 2, PLANE, PACK], BF16, name="w_grp", tag="w_grp", bufs=2 * PASSES, align_bytes=64
-                )
-            rows = w_sb[qk][:, PACK * g : PACK * (g + 1), :].rearrange("p t (r j) -> p j r t", j=2)
-            copy(out=w_grp[(qk, g)][:, j], in_=rows[:, j])
+        def regroup_w(g, qk, base, ch, width, copy):
+            lo = base + qk * HEADS * width
+            copy(
+                out=w_grp[g][:, lo : lo + HEADS * width, :].rearrange("p (h c) t -> p h c t", h=HEADS),
+                in_=w_sb[qk][:, g].rearrange("p t (h c) -> p h c t", h=HEADS)[:, :, ch : ch + width],
+            )
 
-        def quantise_w(qk, g):
+        def quantise_w(g, lo, hi):
             nc.vector.quantize_mx(
-                out=w_codes[:, g, qk, :].bitcast(FP8X4),
-                scales=w_scales[:, g, qk, :],
-                in_=w_grp[(qk, g)][:].rearrange("p j r t -> p (j r t)"),
+                out=w_codes[:, g, lo:hi].bitcast(FP8X4),
+                scales=w_scales[:, g, lo:hi],
+                in_=w_grp[g][:, lo:hi, :].rearrange("p c t -> p (c t)"),
             )
 
         x_grp = {}
         x_codes = {}
         x_scales = {}
 
-        def transpose_pair(pair):
-            b, r = divmod(pair, PAIRS_PER_SEQ)
+        def prepare(n):
+            b, r = divmod(n, PAIRS_PER_SEQ)
             words = x_sb[b][:].bitcast(F32)
-            x_grp[pair] = stage.tile([P, 2 * WORDS], F32, name="x_grp", tag="x_grp", align_bytes=64)
+            x_grp[n] = stage.tile([P, 2, WORDS], F32, name="x_grp", tag="x_grp", align_bytes=64)
             banks = []
             for s in range(2):
-                bank = tpsum.tile([P, 2 * PASSES, P], F32, name="bank_t", tag="bank_t")
-                for a in range(2 * PASSES):
-                    g, u = divmod(a, 2)
-                    lo = (2 * r + s) * WORDS + g * 2 * P
-                    nc.tensor.transpose(bank[:, a, :], words[:, lo + u : lo + 2 * P : 2], ident[:])
+                bank = tpsum.tile([P, PASSES, 2, P], F32, name="bank_t", tag="bank_t")
+                for g in range(PASSES):
+                    for u in range(2):
+                        lo = g * 2 * P
+                        nc.tensor.transpose(bank[:, g, u, :], words[:, 2 * r + s, lo + u : lo + 2 * P : 2], ident[:])
                 banks.append(bank)
-            return banks
-
-        def copy_out(pair, s, bank, copy):
-            copy(
-                out=x_grp[pair][:, s * WORDS : (s + 1) * WORDS].rearrange("p (g k u) -> p g k u", g=PASSES, u=2),
-                in_=bank[:].rearrange("p (g u) k -> p g k u", u=2),
-            )
-
-        def prepare_pair(pair):
-            banks = transpose_pair(pair)
             for s in range(2):
-                copy_out(pair, s, banks[s], nc.scalar.copy)
-
-        def quantise_x(pair):
-            b, r = divmod(pair, PAIRS_PER_SEQ)
-            if r == 0:
-                x_codes[b] = codes.tile([P, TOK_PP * PASSES * P], U32, name="x_codes", tag="x_codes", align_bytes=64)
-                x_scales[b] = codes.tile([P, TOK_PP * PASSES * P], U8, name="x_scales", tag="x_scales", align_bytes=64)
-            lo = r * 2 * PASSES * P
-            nc.vector.quantize_mx(
-                out=x_codes[b][:, lo : lo + 2 * PASSES * P].bitcast(FP8X4),
-                scales=x_scales[b][:, lo : lo + 2 * PASSES * P],
-                in_=x_grp[pair][:].bitcast(BF16),
-            )
-
-        banks_of = {}
-        products_of = {}
-
-        def unit_key(u):
-            b, rest = divmod(u, UNITS_PER_SEQ)
-            qk, r = divmod(rest, PAIRS_PER_SEQ)
-            return b, qk, r
-
-        def matmuls(u):
-            b, qk, r = unit_key(u)
-            bank_e = acc.tile([P, 2 * PLANE], F32, name="bank_e", tag="bank_e")
-            bank_o = acc.tile([P, 2 * PLANE], F32, name="bank_o", tag="bank_o")
-            banks_of[u] = (bank_e, bank_o)
-            for s in range(2):
-                for j in range(2):
-                    for g in range(PASSES):
-                        lo = ((2 * r + s) * PASSES + g) * P
-                        nc.tensor.matmul_mx(
-                            out=banks_of[u][j][:, PLANE * s : PLANE * (s + 1)],
-                            lhsT=x_codes[b][:, lo : lo + P].bitcast(FP8X4),
-                            lhsT_scale=x_scales[b][:, lo : lo + P],
-                            rhs=w_codes[:, g, qk, PLANE * j : PLANE * (j + 1)].bitcast(FP8X4),
-                            rhs_scale=w_scales[:, g, qk, PLANE * j : PLANE * (j + 1)],
-                            start=(g == 0),
-                            stop=(g == PASSES - 1),
-                        )
-
-        def products(u):
-            r = unit_key(u)[2]
-            if u % 2 == 0:
-                first_p = prod.tile([P, 2, HEADS, BLOCK_TOK, HALF], F32, name="first_p", tag="first_p")
-                second_p = prod.tile([P, 2, HEADS, BLOCK_TOK, HALF], F32, name="second_p", tag="second_p")
-                products_of[u // 2] = (first_p, second_p)
-            first_p, second_p = products_of[u // 2]
-            lo = 2 * (u % 2)
-
-            def multiply(dst, j, bank, table):
-                nc.vector.tensor_tensor(
-                    out=dst[:, j, :, lo : lo + 2, :].rearrange("p h t i -> p t h i"),
-                    in0=bank[:].rearrange("p (t h i) -> p t h i", t=2, h=HEADS),
-                    in1=tab[:, table, 2 * r : 2 * r + 2, :].unsqueeze(2).to_broadcast([P, 2, HEADS, HALF]),
-                    op=MULT,
+                nc.scalar.copy(
+                    out=x_grp[n][:, s, :].rearrange("p (g k u) -> p g k u", g=PASSES, u=2),
+                    in_=banks[s][:].rearrange("p g u k -> p g k u"),
                 )
 
-            bank_e, bank_o = banks_of[u]
-            multiply(first_p, 0, bank_e, COS_EVEN)
-            multiply(second_p, 1, bank_e, SIN_ODD)
-            multiply(first_p, 1, bank_o, COS_ODD)
-            multiply(second_p, 0, bank_o, NEG_SIN_EVEN)
+        def quantise_x(n):
+            x_codes[n] = codes.tile([P, 2 * PASSES * P], U32, name="x_codes", tag="x_codes", align_bytes=64)
+            x_scales[n] = codes.tile([P, 2 * PASSES * P], U8, name="x_scales", tag="x_scales", align_bytes=64)
+            nc.vector.quantize_mx(
+                out=x_codes[n][:].bitcast(FP8X4),
+                scales=x_scales[n][:],
+                in_=x_grp[n][:].rearrange("p s w -> p (s w)").bitcast(BF16),
+            )
 
-        def out_rows(k):
-            b, qk, r = unit_key(2 * k)
-            rows = (out_0, out_1)[qk][b].rearrange("h (p t) c -> p h t c", t=TOK_PP)
-            return rows[:, :, 2 * r : 2 * r + BLOCK_TOK, :]
+        banks_a, banks_b, banks_s = {}, {}, {}
 
-        def interleaved(tile_ap):
-            return tile_ap.rearrange("p h t (i j) -> p h (t i) j", j=2)
+        def group(out, k, lo, width):
+            n, s = divmod(k, 2)
+            for g in range(PASSES):
+                at = (s * PASSES + g) * P
+                nc.tensor.matmul_mx(
+                    out=out,
+                    lhsT=x_codes[n][:, at : at + P].bitcast(FP8X4),
+                    lhsT_scale=x_scales[n][:, at : at + P],
+                    rhs=w_codes[:, g, lo : lo + width].bitcast(FP8X4),
+                    rhs_scale=w_scales[:, g, lo : lo + width],
+                    start=(g == 0),
+                    stop=(g == PASSES - 1),
+                )
 
-        def planes(tile_ap):
-            return tile_ap.rearrange("p j h t i -> p h (t i) j")
+        def matmuls_a(k):
+            banks_a[k] = acc.tile([P, ROWS * CA], F32, name="bank_a", tag="bank_a")
+            group(banks_a[k][:], k, LO_A, ROWS * CA)
 
-        def sum_on_gpsimd(k):
-            first_p, second_p = products_of[k]
-            o_sb = opool.tile([P, HEADS, BLOCK_TOK, CHANNELS], F32, name="o_sb", tag="o_sb")
-            nc.gpsimd.tensor_tensor(
-                out=first_p[:].rearrange("p j h t i -> p (j h t i)"),
-                in0=first_p[:].rearrange("p j h t i -> p (j h t i)"),
-                in1=second_p[:].rearrange("p j h t i -> p (j h t i)"),
+        def matmuls_bs(k):
+            n, s = divmod(k, 2)
+            banks_b[k] = acc.tile([P, ROWS * CB], F32, name="bank_b", tag="bank_b")
+            group(banks_b[k][:, 0:256], k, LO_B, 256)
+            group(banks_b[k][:, 256:384], k, LO_B + 256, 128)
+            if s == 0:
+                banks_s[n] = acc.tile([P, 2, ROWS * CS], F32, name="bank_s", tag="bank_s")
+            group(banks_s[n][:, s, :], k, LO_S, ROWS * CS)
+
+        o_sb, p2_sb, s1_sb, s2_sb = {}, {}, {}, {}
+
+        def spot(n):
+            return o_sb[n // 2], 2 * (n % 2)
+
+        def products(k, bank, c0, width):
+            n, s = divmod(k, 2)
+            j = 2 * (n % PAIRS_PER_SEQ) + s
+            if s == 0 and c0 == 0:
+                if n % 2 == 0:
+                    o_sb[n // 2] = opool.tile([P, ROWS, STORE_TOK, CHANNELS], F32, name="o_sb", tag="o_sb")
+                p2_sb[n] = prod.tile([P, ROWS, 2, CV], F32, name="p2", tag="p2")
+            o, t0 = spot(n)
+            nc.vector.tensor_tensor(
+                out=o[:, :, t0 + s, c0 : c0 + width],
+                in0=bank[:].rearrange("p (r c) -> p r c", r=ROWS),
+                in1=cos_f[:, j, c0 : c0 + width].unsqueeze(1).to_broadcast([P, ROWS, width]),
+                op=MULT,
+            )
+            nc.vector.tensor_tensor(
+                out=p2_sb[n][:, :, s, c0 : c0 + width].rearrange("p r (i e) -> p r i e", e=2),
+                in0=bank[:].rearrange("p (r i e) -> p r i e", r=ROWS, e=2)[:, :, :, ::-1],
+                in1=sin_f[:, j, c0 : c0 + width]
+                .rearrange("p (i e) -> p i e", e=2)
+                .unsqueeze(1)
+                .to_broadcast([P, ROWS, width // 2, 2]),
+                op=MULT,
+            )
+
+        def scalar_products(n):
+            s1_sb[n] = prod.tile([P, 2, CS, ROWS], F32, name="s1", tag="s1")
+            s2_sb[n] = prod.tile([P, 2, CS, ROWS], F32, name="s2", tag="s2")
+            for s in range(2):
+                j = 2 * (n % PAIRS_PER_SEQ) + s
+                src = banks_s[n][:, s, :].rearrange("p (r c) -> p c r", c=CS)
+                for c in range(CS):
+                    ch = CV + c
+                    partner = c + 1 - 2 * (c % 2)
+                    nc.scalar.activation(
+                        out=s1_sb[n][:, s, c, :], in_=src[:, c], func=COPY, scale=cos_f[:, j, ch : ch + 1]
+                    )
+                    nc.scalar.activation(
+                        out=s2_sb[n][:, s, c, :], in_=src[:, partner], func=COPY, scale=sin_f[:, j, ch : ch + 1]
+                    )
+
+        def add_s(n):
+            nc.vector.tensor_tensor(
+                out=s1_sb[n][:].rearrange("p s c r -> p (s c r)"),
+                in0=s1_sb[n][:].rearrange("p s c r -> p (s c r)"),
+                in1=s2_sb[n][:].rearrange("p s c r -> p (s c r)"),
                 op=ADD,
             )
-            nc.scalar.copy(out=interleaved(o_sb[:]), in_=planes(first_p[:]))
-            return o_sb
 
-        def sum_on_vector_and_store(k):
-            first_p, second_p = products_of[k]
-            o_sb = opool.tile([P, HEADS, BLOCK_TOK, CHANNELS], F32, name="o_sb", tag="o_sb")
-            for lo in (0, 2):
-                nc.vector.tensor_tensor(
-                    out=interleaved(o_sb[:, :, lo : lo + 2, :]),
-                    in0=planes(first_p[:, :, :, lo : lo + 2, :]),
-                    in1=planes(second_p[:, :, :, lo : lo + 2, :]),
-                    op=ADD,
+        def permute_s(n):
+            o, t0 = spot(n)
+            nc.scalar.copy(
+                out=o[:, :, t0 : t0 + 2, CV:].rearrange("p (r e) s c -> p r s c e", e=2),
+                in_=s1_sb[n][:].rearrange("p s c (r e) -> p r s c e", e=2),
+            )
+
+        def add(n, lo, hi, engine):
+            o, t0 = spot(n)
+            dst = o[:, :, t0 + lo : t0 + hi, 0:CV]
+            engine.tensor_tensor(out=dst, in0=dst, in1=p2_sb[n][:, :, lo:hi, :], op=ADD)
+
+        def store(n, tokens):
+            o, t0 = spot(n)
+            b, r = divmod(n, PAIRS_PER_SEQ)
+            lo = t0 + 2 - tokens
+            at = (2 * r + 2 - tokens) * CHANNELS
+            for qk in range(2):
+                rows = (out_0, out_1)[qk][b].rearrange("h (p t) c -> p h (t c)", t=TOK_PP)
+                nc.sync.dma_start(
+                    out=rows[:, :, at : at + tokens * CHANNELS],
+                    in_=o[:, qk * HEADS : (qk + 1) * HEADS, lo : t0 + 2, :].rearrange("p h t c -> p h (t c)"),
                 )
-                nc.sync.dma_start(out=out_rows(k)[:, :, lo : lo + 2, :], in_=o_sb[:, :, lo : lo + 2, :])
 
-
-        prepare_pair(0)
-        regroup_w(Q, 0, 0, nc.vector.tensor_copy)
-        regroup_w(Q, 0, 1, nc.vector.tensor_copy)
-        regroup_w(Q, 1, 0, nc.vector.tensor_copy)
-        regroup_w(Q, 1, 1, nc.scalar.copy)
+        prepare(0)
+        for g, qk in ((0, 0), (0, 1)):
+            regroup_w(g, qk, LO_A, 0, CA, nc.vector.tensor_copy)
+            regroup_w(g, qk, LO_B, CA, CB, nc.scalar.copy)
+            regroup_w(g, qk, LO_S, CV, CS, nc.scalar.copy)
         quantise_x(0)
-        quantise_w(Q, 0)
-        quantise_w(Q, 1)
-        matmuls(0)
-        regroup_w(K, 0, 0, nc.vector.tensor_copy)
-        regroup_w(K, 0, 1, nc.vector.tensor_copy)
+        regroup_w(1, 0, LO_A, 0, CA, nc.vector.tensor_copy)
+        quantise_w(0, LO_A, LO_B)
+        regroup_w(1, 1, LO_A, 0, CA, nc.vector.tensor_copy)
+        quantise_w(1, LO_A, LO_B)
+        for qk in range(2):
+            regroup_w(1, qk, LO_B, CA, CB, nc.scalar.copy)
+            regroup_w(1, qk, LO_S, CV, CS, nc.scalar.copy)
+        matmuls_a(0)
+        prepare(1)
+        prepare(2)
+        products(0, banks_a[0], 0, CA)
+        for g in range(PASSES):
+            quantise_w(g, LO_B, ROWS * CHANNELS)
+        matmuls_bs(0)
+        matmuls_a(1)
+        matmuls_bs(1)
+        products(0, banks_b[0], CA, CB)
+        quantise_x(1)
 
-        issued = 1
-        held = None
-        for u in range(UNITS):
-            products(u)
-            k = u // 2
-            if u == 0:
-                for pair in range(1, PAIRS_PER_SEQ):
-                    banks = transpose_pair(pair)
-                    copy_out(pair, 0, banks[0], nc.scalar.copy)
-                    copy_out(pair, 1, banks[1], nc.vector.tensor_copy)
-                    quantise_x(pair)
-                regroup_w(K, 1, 0, nc.scalar.copy)
-                regroup_w(K, 1, 1, nc.scalar.copy)
-            if u == FIRST_K_UNIT - 1:
-                quantise_w(K, 0)
-                quantise_w(K, 1)
-            if u % 2 == 1 and PAIRS_PER_SEQ <= k + 3 < PAIRS:
-                quantise_x(k + 3)
-            while issued < UNITS and issued <= u + AHEAD and (issued < FIRST_K_UNIT or u >= FIRST_K_UNIT - 1):
-                matmuls(issued)
-                issued += 1
-            if u == 1:
-                prepare_pair(PAIRS_PER_SEQ)
-            if u % 2 == 1 and k + 5 < PAIRS:
-                prepare_pair(k + 5)
-            if u % 2 == 1:
-                if k < BLOCKS - 2:
-                    o_sb = sum_on_gpsimd(k)
-                    nc.sync.dma_start(out=out_rows(k), in_=o_sb[:])
-                elif k == BLOCKS - 2:
-                    held = sum_on_gpsimd(k)
-                else:
-                    sum_on_vector_and_store(k)
-                    nc.sync.dma_start(out=out_rows(k - 1), in_=held[:])
+        for k in range(1, TILES):
+            n, s = divmod(k, 2)
+            if s == 0 and n >= 2:
+                permute_s(n - 2)
+                if (n - 2) % 2 == 1:
+                    store(n - 2, STORE_TOK)
+            if k + 1 < TILES:
+                matmuls_a(k + 1)
+                matmuls_bs(k + 1)
+            if s == 1:
+                if n + 3 < PAIRS:
+                    prepare(n + 3)
+                scalar_products(n)
+            products(k, banks_a[k], 0, CA)
+            products(k, banks_b[k], CA, CB)
+            if s == 1:
+                if n + 2 < PAIRS:
+                    quantise_x(n + 2)
+                if n > 0:
+                    add_s(n - 1)
+                if n < PAIRS - 1:
+                    add(n, 0, 2, nc.gpsimd)
+            elif n == PAIRS - 1:
+                add(n, 0, 1, nc.vector)
+        last = PAIRS - 1
+        add_s(last)
+        permute_s(last - 1)
+        permute_s(last)
+        add(last, 1, 2, nc.vector)
+        store(last - 1, 2)
+        store(last, 2)

@@ -157,14 +157,15 @@ def tile_multiscaleretention_pa_t_kernel(tc, x, sin, cos, Wq, Wk, out_0, out_1):
             banks_a[k] = acc.tile([P, ROWS * CA], F32, name="bank_a", tag="bank_a")
             group(banks_a[k][:], k, LO_A, ROWS * CA)
 
-        def matmuls_bs(k):
-            n, s = divmod(k, 2)
+        def matmuls_b(k):
             banks_b[k] = acc.tile([P, ROWS * CB], F32, name="bank_b", tag="bank_b")
             group(banks_b[k][:, 0:256], k, LO_B, 256)
             group(banks_b[k][:, 256:384], k, LO_B + 256, 128)
-            if s == 0:
-                banks_s[n] = acc.tile([P, 2, ROWS * CS], F32, name="bank_s", tag="bank_s")
-            group(banks_s[n][:, s, :], k, LO_S, ROWS * CS)
+
+        def matmuls_s(n):
+            banks_s[n] = acc.tile([P, 2, 2, ROWS * CS], F32, name="bank_s", tag="bank_s")
+            for s in range(2):
+                group(banks_s[n][:, 0, s, :], 2 * n + s, LO_S, ROWS * CS)
 
         o_sb, p2_sb, s1_sb, s2_sb = {}, {}, {}, {}
 
@@ -200,7 +201,7 @@ def tile_multiscaleretention_pa_t_kernel(tc, x, sin, cos, Wq, Wk, out_0, out_1):
             s2_sb[n] = prod.tile([P, 2, CS, ROWS], F32, name="s2", tag="s2")
             for s in range(2):
                 j = 2 * (n % PAIRS_PER_SEQ) + s
-                src = banks_s[n][:, s, :].rearrange("p (r c) -> p c r", c=CS)
+                src = banks_s[n][:, 0, s, :].rearrange("p (r c) -> p c r", c=CS)
                 for c in range(CS):
                     ch = CV + c
                     partner = c + 1 - 2 * (c % 2)
@@ -212,18 +213,20 @@ def tile_multiscaleretention_pa_t_kernel(tc, x, sin, cos, Wq, Wk, out_0, out_1):
                     )
 
         def add_s(n):
-            nc.vector.tensor_tensor(
-                out=s1_sb[n][:].rearrange("p s c r -> p (s c r)"),
-                in0=s1_sb[n][:].rearrange("p s c r -> p (s c r)"),
-                in1=s2_sb[n][:].rearrange("p s c r -> p (s c r)"),
-                op=ADD,
-            )
+            for part, rhs in enumerate((s1_sb[n], s2_sb[n])):
+                nc.tensor.matmul(
+                    banks_s[n][:, 1].rearrange("p s q -> p (s q)"),
+                    lhsT=ident[:],
+                    rhs=rhs[:].rearrange("p s c r -> p (s c r)"),
+                    start=(part == 0),
+                    stop=(part == 1),
+                )
 
         def permute_s(n):
             o, t0 = spot(n)
             nc.scalar.copy(
                 out=o[:, :, t0 : t0 + 2, CV:].rearrange("p (r e) s c -> p r s c e", e=2),
-                in_=s1_sb[n][:].rearrange("p s c (r e) -> p r s c e", e=2),
+                in_=banks_s[n][:, 1].rearrange("p s (c r e) -> p r s c e", c=CS, e=2),
             )
 
         def add(n, lo, hi, engine):
@@ -258,44 +261,43 @@ def tile_multiscaleretention_pa_t_kernel(tc, x, sin, cos, Wq, Wk, out_0, out_1):
             regroup_w(1, qk, LO_S, CV, CS, nc.scalar.copy)
         matmuls_a(0)
         prepare(1)
-        prepare(2)
         products(0, banks_a[0], 0, CA)
         for g in range(PASSES):
             quantise_w(g, LO_B, ROWS * CHANNELS)
-        matmuls_bs(0)
+        matmuls_b(0)
         matmuls_a(1)
-        matmuls_bs(1)
+        matmuls_b(1)
+        matmuls_s(0)
+        prepare(2)
         products(0, banks_b[0], CA, CB)
+        add(0, 0, 1, nc.gpsimd)
         quantise_x(1)
 
         for k in range(1, TILES):
             n, s = divmod(k, 2)
-            if s == 0 and n >= 2:
-                permute_s(n - 2)
-                if (n - 2) % 2 == 1:
-                    store(n - 2, STORE_TOK)
+            if s == 0:
+                matmuls_s(n)
+            elif n > 0:
+                permute_s(n - 1)
+                if n % 2 == 0:
+                    store(n - 1, STORE_TOK)
             if k + 1 < TILES:
                 matmuls_a(k + 1)
-                matmuls_bs(k + 1)
-            if s == 1:
-                if n + 3 < PAIRS:
-                    prepare(n + 3)
+                matmuls_b(k + 1)
+            if s == 0:
+                add_s(n - 1)
                 scalar_products(n)
+            elif n == 0:
+                scalar_products(n)
+            if s == 1 and n + 3 < PAIRS:
+                prepare(n + 3)
             products(k, banks_a[k], 0, CA)
             products(k, banks_b[k], CA, CB)
-            if s == 1:
-                if n + 2 < PAIRS:
-                    quantise_x(n + 2)
-                if n > 0:
-                    add_s(n - 1)
-                if n < PAIRS - 1:
-                    add(n, 0, 2, nc.gpsimd)
-            elif n == PAIRS - 1:
-                add(n, 0, 1, nc.vector)
+            if s == 1 and n + 2 < PAIRS:
+                quantise_x(n + 2)
+            add(n, s, s + 1, nc.gpsimd if k < TILES - 1 else nc.vector)
         last = PAIRS - 1
         add_s(last)
-        permute_s(last - 1)
-        permute_s(last)
-        add(last, 1, 2, nc.vector)
         store(last - 1, 2)
+        permute_s(last)
         store(last, 2)

@@ -63,12 +63,13 @@ def tile_multiscaleretention_pa_t_kernel(tc, x, sin, cos, Wq, Wk, out_0, out_1):
         def load_x(b, lo, hi):
             nc.sync.dma_start(out=x_sb[b][:, lo:hi, :], in_=x_dram[b][:, lo:hi, :])
 
-        load_x(0, 0, 2)
+        load_x(0, 0, 1)
         for g in range(PASSES):
             for qk in range(2):
                 nc.sync.dma_start(out=w_sb[qk][:, g], in_=w_dram[qk][:, g])
         nc.sync.dma_start(out=cos_sb[:], in_=cos.rearrange("(p j) c -> p j c", j=TOK_PP))
         nc.sync.dma_start(out=sin_sb[:], in_=sin.rearrange("(p j) c -> p j c", j=TOK_PP))
+        load_x(0, 1, 2)
         load_x(0, 2, 4)
         load_x(0, 4, 8)
         for b in range(1, SEQS):
@@ -110,31 +111,34 @@ def tile_multiscaleretention_pa_t_kernel(tc, x, sin, cos, Wq, Wk, out_0, out_1):
         x_codes = {}
         x_scales = {}
 
-        def prepare(n):
+        def prepare(n, tiles=(0, 1)):
             b, r = divmod(n, PAIRS_PER_SEQ)
             words = x_sb[b][:].bitcast(F32)
-            x_grp[n] = stage.tile([P, 2, WORDS], F32, name="x_grp", tag="x_grp", align_bytes=64)
-            banks = []
-            for s in range(2):
+            if 0 in tiles:
+                x_grp[n] = stage.tile([P, 2, WORDS], F32, name="x_grp", tag="x_grp", align_bytes=64)
+            banks = {}
+            for s in tiles:
                 bank = tpsum.tile([P, PASSES, 2, P], F32, name="bank_t", tag="bank_t")
                 for g in range(PASSES):
                     for u in range(2):
                         lo = g * 2 * P
                         nc.tensor.transpose(bank[:, g, u, :], words[:, 2 * r + s, lo + u : lo + 2 * P : 2], ident[:])
-                banks.append(bank)
-            for s in range(2):
+                banks[s] = bank
+            for s in tiles:
                 nc.scalar.copy(
                     out=x_grp[n][:, s, :].rearrange("p (g k u) -> p g k u", g=PASSES, u=2),
                     in_=banks[s][:].rearrange("p g u k -> p g k u"),
                 )
 
-        def quantise_x(n):
-            x_codes[n] = codes.tile([P, 2 * PASSES * P], U32, name="x_codes", tag="x_codes", align_bytes=64)
-            x_scales[n] = codes.tile([P, 2 * PASSES * P], U8, name="x_scales", tag="x_scales", align_bytes=64)
+        def quantise_x(n, lo=0, hi=2):
+            if lo == 0:
+                x_codes[n] = codes.tile([P, 2 * PASSES * P], U32, name="x_codes", tag="x_codes", align_bytes=64)
+                x_scales[n] = codes.tile([P, 2 * PASSES * P], U8, name="x_scales", tag="x_scales", align_bytes=64)
+            at = slice(lo * PASSES * P, hi * PASSES * P)
             nc.vector.quantize_mx(
-                out=x_codes[n][:].bitcast(FP8X4),
-                scales=x_scales[n][:],
-                in_=x_grp[n][:].rearrange("p s w -> p (s w)").bitcast(BF16),
+                out=x_codes[n][:, at].bitcast(FP8X4),
+                scales=x_scales[n][:, at],
+                in_=x_grp[n][:, lo:hi, :].rearrange("p s w -> p (s w)").bitcast(BF16),
             )
 
         banks_a, banks_b, banks_s = {}, {}, {}
@@ -231,27 +235,27 @@ def tile_multiscaleretention_pa_t_kernel(tc, x, sin, cos, Wq, Wk, out_0, out_1):
 
         def add(n, lo, hi, engine):
             o, t0 = spot(n)
-            dst = o[:, :, t0 + lo : t0 + hi, 0:CV]
-            engine.tensor_tensor(out=dst, in0=dst, in1=p2_sb[n][:, :, lo:hi, :], op=ADD)
+            dst = o[:, lo:hi, t0 : t0 + 2, 0:CV]
+            engine.tensor_tensor(out=dst, in0=dst, in1=p2_sb[n][:, lo:hi], op=ADD)
 
-        def store(n, tokens):
+        def store(n, tokens, which=(0, 1)):
             o, t0 = spot(n)
             b, r = divmod(n, PAIRS_PER_SEQ)
             lo = t0 + 2 - tokens
             at = (2 * r + 2 - tokens) * CHANNELS
-            for qk in range(2):
+            for qk in which:
                 rows = (out_0, out_1)[qk][b].rearrange("h (p t) c -> p h (t c)", t=TOK_PP)
                 nc.sync.dma_start(
                     out=rows[:, :, at : at + tokens * CHANNELS],
                     in_=o[:, qk * HEADS : (qk + 1) * HEADS, lo : t0 + 2, :].rearrange("p h t c -> p h (t c)"),
                 )
 
-        prepare(0)
+        prepare(0, (0,))
         for g, qk in ((0, 0), (0, 1)):
             regroup_w(g, qk, LO_A, 0, CA, nc.vector.tensor_copy)
             regroup_w(g, qk, LO_B, CA, CB, nc.scalar.copy)
             regroup_w(g, qk, LO_S, CV, CS, nc.scalar.copy)
-        quantise_x(0)
+        quantise_x(0, 0, 1)
         regroup_w(1, 0, LO_A, 0, CA, nc.vector.tensor_copy)
         quantise_w(0, LO_A, LO_B)
         regroup_w(1, 1, LO_A, 0, CA, nc.vector.tensor_copy)
@@ -260,17 +264,18 @@ def tile_multiscaleretention_pa_t_kernel(tc, x, sin, cos, Wq, Wk, out_0, out_1):
             regroup_w(1, qk, LO_B, CA, CB, nc.scalar.copy)
             regroup_w(1, qk, LO_S, CV, CS, nc.scalar.copy)
         matmuls_a(0)
+        prepare(0, (1,))
         prepare(1)
         products(0, banks_a[0], 0, CA)
         for g in range(PASSES):
             quantise_w(g, LO_B, ROWS * CHANNELS)
+        quantise_x(0, 1, 2)
         matmuls_b(0)
         matmuls_a(1)
         matmuls_b(1)
         matmuls_s(0)
         prepare(2)
         products(0, banks_b[0], CA, CB)
-        add(0, 0, 1, nc.gpsimd)
         quantise_x(1)
 
         for k in range(1, TILES):
@@ -295,9 +300,12 @@ def tile_multiscaleretention_pa_t_kernel(tc, x, sin, cos, Wq, Wk, out_0, out_1):
             products(k, banks_b[k], CA, CB)
             if s == 1 and n + 2 < PAIRS:
                 quantise_x(n + 2)
-            add(n, s, s + 1, nc.gpsimd if k < TILES - 1 else nc.vector)
+            if s == 1 and n + 1 < PAIRS:
+                add(n, 0, ROWS, nc.gpsimd)
         last = PAIRS - 1
         add_s(last)
         store(last - 1, 2)
         permute_s(last)
-        store(last, 2)
+        for qk in range(2):
+            add(last, qk * HEADS, (qk + 1) * HEADS, nc.vector)
+            store(last, 2, (qk,))

from contextlib import ExitStack

import concourse.mybir as mybir
from concourse.masks import make_identity

F32 = mybir.dt.float32
BF16 = mybir.dt.bfloat16
U32 = mybir.dt.uint32
U8 = mybir.dt.uint8
FP8X4 = mybir.dt.float8_e4m3fn_x4
MULT = mybir.AluOpType.mult
ADD = mybir.AluOpType.add
COPY = mybir.ActivationFunctionType.Copy

P = 128
SEQS, TOKENS, E = 4, 1024, 1024
HEADS, CHANNELS = 8, 64
COLS = HEADS * CHANNELS
ROWS = 2 * HEADS
TOK_PP = TOKENS // P
WORDS = E // 2
PASSES = 2
PACK = 4
PAIRS_PER_SEQ = TOK_PP // 2
PAIRS = SEQS * PAIRS_PER_SEQ
TILES = 2 * PAIRS
STORE_TOK = 4
CA, CB, CS = 32, 24, 8
CV = CA + CB
LO_A, LO_B, LO_S = 0, ROWS * CA, ROWS * CV

FLOPS = 2 * SEQS * TOKENS * E * 2 * COLS


def tile_multiscaleretention_pa_t_kernel(tc, x, sin, cos, Wq, Wk, out_0, out_1):
    nc = tc.nc
    with ExitStack() as ctx:
        const = ctx.enter_context(tc.tile_pool(name="const", bufs=1))
        xpool = ctx.enter_context(tc.tile_pool(name="xpool", bufs=SEQS))
        stage = ctx.enter_context(tc.tile_pool(name="stage", bufs=4))
        codes = ctx.enter_context(tc.tile_pool(name="codes", bufs=4))
        prod = ctx.enter_context(tc.tile_pool(name="prod", bufs=3))
        opool = ctx.enter_context(tc.tile_pool(name="opool", bufs=4))
        tpsum = ctx.enter_context(tc.psum_pool(name="tpsum", bufs=2))
        acc = ctx.enter_context(tc.psum_pool(name="acc", bufs=2))

        ident = const.tile([P, P], F32, name="ident")
        make_identity(nc, ident[:])
        ctx.enter_context(tc.manual_schedule())

        warm_in = const.tile([P, 8], F32, name="warm_in")
        warm_out = const.tile([P, 8], F32, name="warm_out")
        nc.vector.memset(warm_in[:], 0.0)
        nc.scalar.activation(out=warm_out[:], in_=warm_in[:], func=COPY, scale=warm_in[:, 0:1])

        x_sb = [xpool.tile([P, TOK_PP, E], BF16, name="x_sb", tag="x_sb") for b in range(SEQS)]
        x_dram = [x[b].rearrange("(p j) k -> p j k", j=TOK_PP) for b in range(SEQS)]
        w_sb = [const.tile([P, PASSES, PACK, COLS], BF16, name="w_sb%d" % qk) for qk in range(2)]
        w_dram = [w.rearrange("(g p t) c -> p g t c", g=PASSES, p=P, t=PACK) for w in (Wq, Wk)]
        cos_sb = const.tile([P, TOK_PP, CHANNELS], BF16, name="cos_sb")
        sin_sb = const.tile([P, TOK_PP, CHANNELS], BF16, name="sin_sb")

        def load_x(b, lo, hi):
            nc.sync.dma_start(out=x_sb[b][:, lo:hi, :], in_=x_dram[b][:, lo:hi, :])

        load_x(0, 0, 1)
        for g in range(PASSES):
            for qk in range(2):
                nc.sync.dma_start(out=w_sb[qk][:, g], in_=w_dram[qk][:, g])
        nc.sync.dma_start(out=cos_sb[:], in_=cos.rearrange("(p j) c -> p j c", j=TOK_PP))
        nc.sync.dma_start(out=sin_sb[:], in_=sin.rearrange("(p j) c -> p j c", j=TOK_PP))
        load_x(0, 1, 2)
        load_x(0, 2, 4)
        load_x(0, 4, 8)
        for b in range(1, SEQS):
            load_x(b, 0, 4)
            load_x(b, 4, 8)

        cos_f = const.tile([P, TOK_PP, CHANNELS], F32, name="cos_f")
        sin_f = const.tile([P, TOK_PP, CHANNELS], F32, name="sin_f")
        nc.gpsimd.tensor_scalar(out=cos_f[:], in0=cos_sb[:], scalar1=1.0, scalar2=0.0, op0=MULT, op1=ADD)
        for par, sign in ((0, -1.0), (1, 1.0)):
            nc.gpsimd.tensor_scalar(
                out=sin_f[:].rearrange("p t (i e) -> p e t i", e=2)[:, par],
                in0=sin_sb[:].rearrange("p t (i e) -> p e t i", e=2)[:, par],
                scalar1=sign,
                scalar2=0.0,
                op0=MULT,
                op1=ADD,
            )

        w_grp = [const.tile([P, ROWS * CHANNELS, PACK], BF16, name="w_grp%d" % g, align_bytes=64) for g in range(PASSES)]
        w_codes = const.tile([P, PASSES, ROWS * CHANNELS], U32, name="w_codes", align_bytes=64)
        w_scales = const.tile([P, PASSES, ROWS * CHANNELS], U8, name="w_scales", align_bytes=64)

        def regroup_w(g, qk, base, ch, width, copy):
            lo = base + qk * HEADS * width
            copy(
                out=w_grp[g][:, lo : lo + HEADS * width, :].rearrange("p (h c) t -> p h c t", h=HEADS),
                in_=w_sb[qk][:, g].rearrange("p t (h c) -> p h c t", h=HEADS)[:, :, ch : ch + width],
            )

        def quantise_w(g, lo, hi):
            nc.vector.quantize_mx(
                out=w_codes[:, g, lo:hi].bitcast(FP8X4),
                scales=w_scales[:, g, lo:hi],
                in_=w_grp[g][:, lo:hi, :].rearrange("p c t -> p (c t)"),
            )

        x_grp = {}
        x_codes = {}
        x_scales = {}

        def prepare(n, tiles=(0, 1)):
            b, r = divmod(n, PAIRS_PER_SEQ)
            words = x_sb[b][:].bitcast(F32)
            if 0 in tiles:
                x_grp[n] = stage.tile([P, 2, WORDS], F32, name="x_grp", tag="x_grp", align_bytes=64)
            banks = {}
            for s in tiles:
                bank = tpsum.tile([P, PASSES, 2, P], F32, name="bank_t", tag="bank_t")
                for g in range(PASSES):
                    for u in range(2):
                        lo = g * 2 * P
                        nc.tensor.transpose(bank[:, g, u, :], words[:, 2 * r + s, lo + u : lo + 2 * P : 2], ident[:])
                banks[s] = bank
            for s in tiles:
                nc.scalar.copy(
                    out=x_grp[n][:, s, :].rearrange("p (g k u) -> p g k u", g=PASSES, u=2),
                    in_=banks[s][:].rearrange("p g u k -> p g k u"),
                )

        def quantise_x(n, lo=0, hi=2):
            if lo == 0:
                x_codes[n] = codes.tile([P, 2 * PASSES * P], U32, name="x_codes", tag="x_codes", align_bytes=64)
                x_scales[n] = codes.tile([P, 2 * PASSES * P], U8, name="x_scales", tag="x_scales", align_bytes=64)
            at = slice(lo * PASSES * P, hi * PASSES * P)
            nc.vector.quantize_mx(
                out=x_codes[n][:, at].bitcast(FP8X4),
                scales=x_scales[n][:, at],
                in_=x_grp[n][:, lo:hi, :].rearrange("p s w -> p (s w)").bitcast(BF16),
            )

        banks_a, banks_b, banks_s = {}, {}, {}

        def group(out, k, lo, width):
            n, s = divmod(k, 2)
            for g in range(PASSES):
                at = (s * PASSES + g) * P
                nc.tensor.matmul_mx(
                    out=out,
                    lhsT=x_codes[n][:, at : at + P].bitcast(FP8X4),
                    lhsT_scale=x_scales[n][:, at : at + P],
                    rhs=w_codes[:, g, lo : lo + width].bitcast(FP8X4),
                    rhs_scale=w_scales[:, g, lo : lo + width],
                    start=(g == 0),
                    stop=(g == PASSES - 1),
                )

        def matmuls_a(k):
            banks_a[k] = acc.tile([P, ROWS * CA], F32, name="bank_a", tag="bank_a")
            group(banks_a[k][:], k, LO_A, ROWS * CA)

        def matmuls_b(k):
            banks_b[k] = acc.tile([P, ROWS * CB], F32, name="bank_b", tag="bank_b")
            group(banks_b[k][:, 0:256], k, LO_B, 256)
            group(banks_b[k][:, 256:384], k, LO_B + 256, 128)

        def matmuls_s(n):
            banks_s[n] = acc.tile([P, 2, 2, ROWS * CS], F32, name="bank_s", tag="bank_s")
            for s in range(2):
                group(banks_s[n][:, 0, s, :], 2 * n + s, LO_S, ROWS * CS)

        o_sb, p2_sb, s1_sb, s2_sb = {}, {}, {}, {}

        def spot(n):
            return o_sb[n // 2], 2 * (n % 2)

        def products(k, bank, c0, width):
            n, s = divmod(k, 2)
            j = 2 * (n % PAIRS_PER_SEQ) + s
            if s == 0 and c0 == 0:
                if n % 2 == 0:
                    o_sb[n // 2] = opool.tile([P, ROWS, STORE_TOK, CHANNELS], F32, name="o_sb", tag="o_sb")
                p2_sb[n] = prod.tile([P, ROWS, 2, CV], F32, name="p2", tag="p2")
            o, t0 = spot(n)
            nc.vector.tensor_tensor(
                out=o[:, :, t0 + s, c0 : c0 + width],
                in0=bank[:].rearrange("p (r c) -> p r c", r=ROWS),
                in1=cos_f[:, j, c0 : c0 + width].unsqueeze(1).to_broadcast([P, ROWS, width]),
                op=MULT,
            )
            nc.vector.tensor_tensor(
                out=p2_sb[n][:, :, s, c0 : c0 + width].rearrange("p r (i e) -> p r i e", e=2),
                in0=bank[:].rearrange("p (r i e) -> p r i e", r=ROWS, e=2)[:, :, :, ::-1],
                in1=sin_f[:, j, c0 : c0 + width]
                .rearrange("p (i e) -> p i e", e=2)
                .unsqueeze(1)
                .to_broadcast([P, ROWS, width // 2, 2]),
                op=MULT,
            )

        def scalar_products(n):
            s1_sb[n] = prod.tile([P, 2, CS, ROWS], F32, name="s1", tag="s1")
            s2_sb[n] = prod.tile([P, 2, CS, ROWS], F32, name="s2", tag="s2")
            for s in range(2):
                j = 2 * (n % PAIRS_PER_SEQ) + s
                src = banks_s[n][:, 0, s, :].rearrange("p (r c) -> p c r", c=CS)
                for c in range(CS):
                    ch = CV + c
                    partner = c + 1 - 2 * (c % 2)
                    nc.scalar.activation(
                        out=s1_sb[n][:, s, c, :], in_=src[:, c], func=COPY, scale=cos_f[:, j, ch : ch + 1]
                    )
                    nc.scalar.activation(
                        out=s2_sb[n][:, s, c, :], in_=src[:, partner], func=COPY, scale=sin_f[:, j, ch : ch + 1]
                    )

        def add_s(n):
            for part, rhs in enumerate((s1_sb[n], s2_sb[n])):
                nc.tensor.matmul(
                    banks_s[n][:, 1].rearrange("p s q -> p (s q)"),
                    lhsT=ident[:],
                    rhs=rhs[:].rearrange("p s c r -> p (s c r)"),
                    start=(part == 0),
                    stop=(part == 1),
                )

        def permute_s(n):
            o, t0 = spot(n)
            nc.scalar.copy(
                out=o[:, :, t0 : t0 + 2, CV:].rearrange("p (r e) s c -> p r s c e", e=2),
                in_=banks_s[n][:, 1].rearrange("p s (c r e) -> p r s c e", c=CS, e=2),
            )

        def add(n, lo, hi, engine):
            o, t0 = spot(n)
            dst = o[:, lo:hi, t0 : t0 + 2, 0:CV]
            engine.tensor_tensor(out=dst, in0=dst, in1=p2_sb[n][:, lo:hi], op=ADD)

        def store(n, tokens, which=(0, 1)):
            o, t0 = spot(n)
            b, r = divmod(n, PAIRS_PER_SEQ)
            lo = t0 + 2 - tokens
            at = (2 * r + 2 - tokens) * CHANNELS
            for qk in which:
                rows = (out_0, out_1)[qk][b].rearrange("h (p t) c -> p h (t c)", t=TOK_PP)
                nc.sync.dma_start(
                    out=rows[:, :, at : at + tokens * CHANNELS],
                    in_=o[:, qk * HEADS : (qk + 1) * HEADS, lo : t0 + 2, :].rearrange("p h t c -> p h (t c)"),
                )

        prepare(0, (0,))
        for g, qk in ((0, 0), (0, 1)):
            regroup_w(g, qk, LO_A, 0, CA, nc.vector.tensor_copy)
            regroup_w(g, qk, LO_B, CA, CB, nc.scalar.copy)
            regroup_w(g, qk, LO_S, CV, CS, nc.scalar.copy)
        quantise_x(0, 0, 1)
        regroup_w(1, 0, LO_A, 0, CA, nc.vector.tensor_copy)
        quantise_w(0, LO_A, LO_B)
        regroup_w(1, 1, LO_A, 0, CA, nc.vector.tensor_copy)
        quantise_w(1, LO_A, LO_B)
        for qk in range(2):
            regroup_w(1, qk, LO_B, CA, CB, nc.scalar.copy)
            regroup_w(1, qk, LO_S, CV, CS, nc.scalar.copy)
        matmuls_a(0)
        prepare(0, (1,))
        prepare(1)
        products(0, banks_a[0], 0, CA)
        for g in range(PASSES):
            quantise_w(g, LO_B, ROWS * CHANNELS)
        quantise_x(0, 1, 2)
        matmuls_b(0)
        matmuls_a(1)
        matmuls_b(1)
        matmuls_s(0)
        prepare(2)
        products(0, banks_b[0], CA, CB)
        quantise_x(1)

        for k in range(1, TILES):
            n, s = divmod(k, 2)
            if s == 0:
                matmuls_s(n)
            elif n > 0:
                permute_s(n - 1)
                if n % 2 == 0:
                    store(n - 1, STORE_TOK)
            if k + 1 < TILES:
                matmuls_a(k + 1)
                matmuls_b(k + 1)
            if s == 0:
                add_s(n - 1)
                scalar_products(n)
            elif n == 0:
                scalar_products(n)
            if s == 1 and n + 3 < PAIRS:
                prepare(n + 3)
            products(k, banks_a[k], 0, CA)
            products(k, banks_b[k], CA, CB)
            if s == 1 and n + 2 < PAIRS:
                quantise_x(n + 2)
            if s == 1 and n + 1 < PAIRS:
                add(n, 0, ROWS, nc.gpsimd)
        last = PAIRS - 1
        add_s(last)
        store(last - 1, 2)
        permute_s(last)
        for qk in range(2):
            add(last, qk * HEADS, (qk + 1) * HEADS, nc.vector)
            store(last, 2, (qk,))
